import numpy as np
import ml_dtypes

BF16 = ml_dtypes.bfloat16


def bf(x):
    return np.asarray(x, np.float32).astype(BF16)


def f32(x):
    return np.asarray(x, np.float32)


def f64(x):
    return np.asarray(x).astype(np.float64)


def striped(idx):
    return np.tile(idx.reshape(-1, 16).T, (8, 1))


C, S, N, G, K = 128, 256, 128, 16, 3
RES = 0.5
DIM = 23.5
CENTER = DIM / 2.0 - (G - 1) * RES / 2.0
ORIGIN = CENTER - DIM / 2.0


def density(coords, radii):
    ax = ORIGIN + RES * np.arange(G)
    dx2 = (ax[None, :] - coords[:, 0:1]) ** 2
    dy2 = (ax[None, :] - coords[:, 1:2]) ** 2
    dz2 = (ax[None, :] - coords[:, 2:3]) ** 2
    d2 = (dx2[:, :, None, None] + dy2[:, None, :, None] + dz2[:, None, None, :]).reshape(C, G * G * G)
    q = d2 / (radii * radii)
    u = np.sqrt(q)
    return np.where(u < 1.0, np.exp(-2.0 * q), np.where(u < 1.5, np.exp(-2.0) * (4.0 * q - 12.0 * u + 9.0), 0.0))


def setup_inputs():
    return {"coords": f32(2.5 * np.random.standard_normal((C, K))), "radii": f32(1.0 + 0.8 * np.random.uniform(size=(C, 1))), "types": f32(bf(np.random.uniform(size=(C, S)))), "offs": striped(np.random.permutation(S)[:N])}


def reference(coords, radii, types, offs):
    idx = offs[:16].T.reshape(-1)
    dens = density(f64(coords), f64(radii))
    return f64(types)[:, idx].T @ dens

@@ -1,0 +1,181 @@
+import math
+
+import concourse.mybir as mybir
+
+F32 = mybir.dt.float32
+BF16 = mybir.dt.bfloat16
+U16 = mybir.dt.uint16
+ALU = mybir.AluOpType
+FN = mybir.ActivationFunctionType
+
+ATOMS = 128
+CHANNELS = 256
+PICKED = 128
+G = 16
+SLAB = G * G
+POINTS = G * SLAB
+PSUM_BANKS = 8
+LEAD = 4
+
+GRID_ORIGIN = -3.75
+GRID_STEP = 0.5
+Q_CORE = 1.0
+Q_END = 2.25
+
+DEGREE = 6
+CENTER = Q_CORE / 2.0
+STEPS = DEGREE + 1
+
+FLOPS = 2 * ATOMS * PICKED * POINTS
+
+
+def power_coefficient(k):
+    rest = sum(CENTER**m / math.factorial(m) for m in range(DEGREE - k + 1))
+    return (-1.0) ** k / math.factorial(k) * math.exp(-CENTER) * rest
+
+
+def tile_coords2grid_kernel(tc, coords, radii, types, offs, out):
+    nc = tc.nc
+    with (
+        tc.tile_pool(name="held", bufs=1) as held,
+        tc.psum_pool(name="psum", bufs=PSUM_BANKS) as psum,
+    ):
+        xyz = held.tile([ATOMS, 3], F32)
+        nc.sync.dma_start(xyz[:], coords)
+        radius = held.tile([ATOMS, 1], F32)
+        nc.scalar.dma_start(radius[:], radii)
+        offsets = held.tile([ATOMS, PICKED // 16], U16)
+        nc.sync.dma_start(offsets[:], offs)
+        table = held.tile([ATOMS, CHANNELS], F32)
+        nc.scalar.dma_start(table[:], types)
+
+        unit = held.tile([ATOMS, G], F32)
+        nc.vector.memset(unit[:], 1.0)
+        pitch = held.tile([ATOMS, G], F32)
+        nc.vector.memset(pitch[:], GRID_STEP)
+        axis = held.tile([ATOMS, G], F32)
+        nc.vector.tensor_tensor_scan(axis[:], unit[:], pitch[:], GRID_ORIGIN - GRID_STEP, ALU.mult, ALU.add)
+
+        one = held.tile([ATOMS, 1], F32)
+        nc.vector.memset(one[:], 1.0)
+        warm = held.tile([ATOMS, 1], F32)
+        nc.scalar.activation(warm[:], one[:], FN.Sqrt)
+
+        series = held.tile([ATOMS, STEPS], F32)
+        for step in range(STEPS):
+            nc.vector.memset(series[:, step : step + 1], power_coefficient(DEGREE - step))
+        coefficient = held.tile([ATOMS, 3 * G, STEPS], F32)
+        nc.vector.tensor_copy(coefficient[:], series[:].unsqueeze(1).to_broadcast([ATOMS, 3 * G, STEPS]))
+        factor = held.tile([ATOMS, 3 * G, STEPS], F32)
+        nc.vector.memset(factor[:], 0.0)
+
+        dist2 = held.tile([ATOMS, 3, G], F32)
+        for k in range(3):
+            nc.scalar.activation(dist2[:, k, :], axis[:], FN.Square, bias=xyz[:, k : k + 1], scale=-1.0)
+        dist2_x = dist2[:, 0, :]
+        core2 = held.tile([ATOMS, 1], F32)
+        nc.vector.scalar_tensor_tensor(core2[:], radius[:], Q_CORE, radius[:], op0=ALU.mult, op1=ALU.mult)
+        end2 = held.tile([ATOMS, 1], F32)
+        nc.vector.scalar_tensor_tensor(end2[:], radius[:], Q_END, radius[:], op0=ALU.mult, op1=ALU.mult)
+        minus_yz = held.tile([ATOMS, SLAB], F32)
+        nc.vector.scalar_tensor_tensor(
+            minus_yz[:].rearrange("n (y z) -> n y z", y=G),
+            dist2[:, 1, :].unsqueeze(2).to_broadcast([ATOMS, G, G]),
+            -1.0,
+            dist2[:, 2, :].unsqueeze(1).to_broadcast([ATOMS, G, G]),
+            op0=ALU.mult,
+            op1=ALU.subtract,
+        )
+        low = held.tile([ATOMS, G], F32)
+        nc.vector.tensor_scalar(low[:], dist2_x, end2[:], 0.0, ALU.subtract, ALU.min)
+        high = held.tile([ATOMS, G], F32)
+        nc.vector.tensor_scalar_sub(high[:], dist2_x, core2[:])
+        inv_radius2 = held.tile([ATOMS, 1], F32)
+        nc.vector.reciprocal(inv_radius2[:], core2[:])
+        minus_inv_radius2 = held.tile([ATOMS, 1], F32)
+        nc.vector.tensor_scalar_mul(minus_inv_radius2[:], inv_radius2[:], -1.0)
+        q_x = held.tile([ATOMS, G], F32)
+        nc.vector.tensor_scalar(q_x[:], dist2_x, end2[:], inv_radius2[:], ALU.min, ALU.mult)
+
+        clamped = held.tile([ATOMS, POINTS], F32)
+        u_clamped = held.tile([ATOMS, POINTS], F32)
+        tail = held.tile([ATOMS, POINTS], F32)
+        dens = held.tile([ATOMS, POINTS], BF16)
+        staged = held.tile([PICKED, POINTS], F32)
+        slabs = [slice(gx * SLAB, (gx + 1) * SLAB) for gx in range(G)]
+
+        def root(gx):
+            nc.vector.tensor_scalar(
+                clamped[:, slabs[gx]], minus_yz[:], low[:, gx : gx + 1], high[:, gx : gx + 1], ALU.max, ALU.min
+            )
+            nc.scalar.activation(
+                u_clamped[:, slabs[gx]],
+                clamped[:, slabs[gx]],
+                FN.Sqrt,
+                bias=q_x[:, gx : gx + 1],
+                scale=minus_inv_radius2[:],
+            )
+
+        for gx in range(LEAD):
+            root(gx)
+
+        picked = held.tile([ATOMS, PICKED], F32)
+        nc.scalar.activation(picked[:], table[:].indirect(offsets[:]), FN.Copy)
+        weights = held.tile([ATOMS, PICKED], BF16)
+        nc.vector.tensor_copy(weights[:], picked[:])
+
+        nc.vector.tensor_scalar(
+            factor[:, :, 1:STEPS],
+            dist2[:].rearrange("n k g -> n (k g)").unsqueeze(2).to_broadcast([ATOMS, 3 * G, DEGREE]),
+            end2[:],
+            inv_radius2[:],
+            ALU.min,
+            ALU.mult,
+        )
+        horner = held.tile([ATOMS, 3, G, STEPS], F32)
+        nc.vector.tensor_tensor_scan(
+            horner[:].rearrange("n k g s -> n (k g s)"),
+            factor[:].rearrange("n t s -> n (t s)"),
+            coefficient[:].rearrange("n t s -> n (t s)"),
+            0.0,
+            ALU.mult,
+            ALU.add,
+        )
+        decay_x = horner[:, 0, :, DEGREE]
+        tail_scale = held.tile([ATOMS, G], F32)
+        nc.vector.tensor_scalar_mul(tail_scale[:], decay_x, 2.0)
+        tail_bias = held.tile([ATOMS, G], F32)
+        nc.vector.tensor_scalar_mul(tail_bias[:], decay_x, -3.0)
+        gauss_axis = held.tile([ATOMS, 2, G], F32)
+        nc.vector.tensor_tensor(gauss_axis[:], horner[:, 1:3, :, DEGREE], horner[:, 1:3, :, DEGREE], ALU.mult)
+        growth_x = held.tile([ATOMS, G], F32)
+        nc.vector.reciprocal(growth_x[:], decay_x)
+        gauss_yz = held.tile([ATOMS, SLAB], F32)
+        nc.vector.tensor_tensor(
+            gauss_yz[:].rearrange("n (y z) -> n y z", y=G),
+            gauss_axis[:, 0, :].unsqueeze(2).to_broadcast([ATOMS, G, G]),
+            gauss_axis[:, 1, :].unsqueeze(1).to_broadcast([ATOMS, G, G]),
+            ALU.mult,
+        )
+        floor_x = held.tile([ATOMS, G], F32)
+        nc.vector.scalar_tensor_tensor(
+            floor_x[:], growth_x[:], math.exp(-2.0 * Q_CORE), growth_x[:], op0=ALU.mult, op1=ALU.mult
+        )
+
+        for gx in range(G):
+            if gx + LEAD < G:
+                root(gx + LEAD)
+            nc.scalar.activation(
+                tail[:, slabs[gx]],
+                u_clamped[:, slabs[gx]],
+                FN.Square,
+                bias=tail_bias[:, gx : gx + 1],
+                scale=tail_scale[:, gx : gx + 1],
+            )
+            nc.vector.scalar_tensor_tensor(
+                dens[:, slabs[gx]], gauss_yz[:], floor_x[:, gx : gx + 1], tail[:, slabs[gx]], op0=ALU.max, op1=ALU.mult
+            )
+            sums = psum.tile([PICKED, SLAB], F32)
+            nc.tensor.matmul(sums[:], weights[:], dens[:, slabs[gx]], start=True, stop=True)
+            nc.any.tensor_copy(staged[:, slabs[gx]], sums[:])
+            nc.sync.dma_start(out[:, slabs[gx]], staged[:, slabs[gx]])

@@ -14,13 +14,15 @@ PICKED = 128
 G = 16
 SLAB = G * G
 POINTS = G * SLAB
-PSUM_BANKS = 8
+PAIR = 2 * SLAB
+PAIRS = POINTS // PAIR
 LEAD = 4
 
 GRID_ORIGIN = -3.75
 GRID_STEP = 0.5
 Q_CORE = 1.0
 Q_END = 2.25
+FLOOR = math.exp(-2.0 * Q_CORE)
 
 DEGREE = 6
 CENTER = Q_CORE / 2.0
@@ -38,7 +40,7 @@ def tile_coords2grid_kernel(tc, coords, radii, types, offs, out):
     nc = tc.nc
     with (
         tc.tile_pool(name="held", bufs=1) as held,
-        tc.psum_pool(name="psum", bufs=PSUM_BANKS) as psum,
+        tc.psum_pool(name="psum", bufs=PAIRS) as psum,
     ):
         xyz = held.tile([ATOMS, 3], F32)
         nc.sync.dma_start(xyz[:], coords)
@@ -68,6 +70,13 @@ def tile_coords2grid_kernel(tc, coords, radii, types, offs, out):
         nc.vector.tensor_copy(coefficient[:], series[:].unsqueeze(1).to_broadcast([ATOMS, 3 * G, STEPS]))
         factor = held.tile([ATOMS, 3 * G, STEPS], F32)
         nc.vector.memset(factor[:], 0.0)
+
+        nothing = held.tile([ATOMS, 1], F32)
+        nc.vector.memset(nothing[:], 0.0)
+        minus_floor = held.tile([ATOMS, PAIR], BF16)
+        nc.vector.tensor_scalar(
+            minus_floor[:], nothing[:].to_broadcast([ATOMS, PAIR]), FLOOR, -1.0, ALU.max, ALU.mult
+        )
 
         dist2 = held.tile([ATOMS, 3, G], F32)
         for k in range(3):
@@ -99,10 +108,11 @@ def tile_coords2grid_kernel(tc, coords, radii, types, offs, out):
 
         clamped = held.tile([ATOMS, POINTS], F32)
         u_clamped = held.tile([ATOMS, POINTS], F32)
-        tail = held.tile([ATOMS, POINTS], F32)
-        dens = held.tile([ATOMS, POINTS], BF16)
+        tail = held.tile([ATOMS, POINTS], BF16)
+        core = held.tile([ATOMS, POINTS], BF16)
         staged = held.tile([PICKED, POINTS], F32)
         slabs = [slice(gx * SLAB, (gx + 1) * SLAB) for gx in range(G)]
+        pairs = [slice(pair * PAIR, (pair + 1) * PAIR) for pair in range(PAIRS)]
 
         def root(gx):
             nc.vector.tensor_scalar(
@@ -124,6 +134,10 @@ def tile_coords2grid_kernel(tc, coords, radii, types, offs, out):
         weights = held.tile([ATOMS, PICKED], BF16)
         nc.vector.tensor_copy(weights[:], picked[:])
 
+        sums = [psum.tile([PICKED, PAIR], F32, name="sums") for pair in range(PAIRS)]
+        for pair in range(PAIRS):
+            nc.tensor.matmul(sums[pair][:], weights[:], minus_floor[:], start=True, stop=False)
+
         nc.vector.tensor_scalar(
             factor[:, :, 1:STEPS],
             dist2[:].rearrange("n k g -> n (k g)").unsqueeze(2).to_broadcast([ATOMS, 3 * G, DEGREE]),
@@ -141,41 +155,32 @@ def tile_coords2grid_kernel(tc, coords, radii, types, offs, out):
             ALU.mult,
             ALU.add,
         )
-        decay_x = horner[:, 0, :, DEGREE]
-        tail_scale = held.tile([ATOMS, G], F32)
-        nc.vector.tensor_scalar_mul(tail_scale[:], decay_x, 2.0)
-        tail_bias = held.tile([ATOMS, G], F32)
-        nc.vector.tensor_scalar_mul(tail_bias[:], decay_x, -3.0)
-        gauss_axis = held.tile([ATOMS, 2, G], F32)
-        nc.vector.tensor_tensor(gauss_axis[:], horner[:, 1:3, :, DEGREE], horner[:, 1:3, :, DEGREE], ALU.mult)
-        growth_x = held.tile([ATOMS, G], F32)
-        nc.vector.reciprocal(growth_x[:], decay_x)
+        gauss_axis = held.tile([ATOMS, 3, G], F32)
+        nc.vector.tensor_tensor(gauss_axis[:], horner[:, :, :, DEGREE], horner[:, :, :, DEGREE], ALU.mult)
+        gauss_x = gauss_axis[:, 0, :]
         gauss_yz = held.tile([ATOMS, SLAB], F32)
         nc.vector.tensor_tensor(
             gauss_yz[:].rearrange("n (y z) -> n y z", y=G),
-            gauss_axis[:, 0, :].unsqueeze(2).to_broadcast([ATOMS, G, G]),
-            gauss_axis[:, 1, :].unsqueeze(1).to_broadcast([ATOMS, G, G]),
+            gauss_axis[:, 1, :].unsqueeze(2).to_broadcast([ATOMS, G, G]),
+            gauss_axis[:, 2, :].unsqueeze(1).to_broadcast([ATOMS, G, G]),
             ALU.mult,
         )
-        floor_x = held.tile([ATOMS, G], F32)
-        nc.vector.scalar_tensor_tensor(
-            floor_x[:], growth_x[:], math.exp(-2.0 * Q_CORE), growth_x[:], op0=ALU.mult, op1=ALU.mult
-        )
 
-        for gx in range(G):
-            if gx + LEAD < G:
-                root(gx + LEAD)
+        for pair in range(PAIRS):
+            for gx in (2 * pair, 2 * pair + 1):
+                if gx + LEAD < G:
+                    root(gx + LEAD)
+                nc.vector.tensor_scalar(
+                    core[:, slabs[gx]], gauss_yz[:], gauss_x[:, gx : gx + 1], FLOOR, ALU.mult, ALU.max
+                )
+            nc.tensor.matmul(sums[pair][:], weights[:], core[:, pairs[pair]], start=False, stop=False)
             nc.scalar.activation(
-                tail[:, slabs[gx]],
-                u_clamped[:, slabs[gx]],
+                tail[:, pairs[pair]],
+                u_clamped[:, pairs[pair]],
                 FN.Square,
-                bias=tail_bias[:, gx : gx + 1],
-                scale=tail_scale[:, gx : gx + 1],
+                bias=3.0 * math.sqrt(FLOOR),
+                scale=-2.0 * math.sqrt(FLOOR),
             )
-            nc.vector.scalar_tensor_tensor(
-                dens[:, slabs[gx]], gauss_yz[:], floor_x[:, gx : gx + 1], tail[:, slabs[gx]], op0=ALU.max, op1=ALU.mult
-            )
-            sums = psum.tile([PICKED, SLAB], F32)
-            nc.tensor.matmul(sums[:], weights[:], dens[:, slabs[gx]], start=True, stop=True)
-            nc.any.tensor_copy(staged[:, slabs[gx]], sums[:])
-            nc.sync.dma_start(out[:, slabs[gx]], staged[:, slabs[gx]])
+            nc.tensor.matmul(sums[pair][:], weights[:], tail[:, pairs[pair]], start=False, stop=True)
+            nc.any.tensor_copy(staged[:, pairs[pair]], sums[pair][:])
+            nc.sync.dma_start(out[:, pairs[pair]], staged[:, pairs[pair]])

@@ -15,8 +15,9 @@ G = 16
 SLAB = G * G
 POINTS = G * SLAB
 PAIR = 2 * SLAB
-PAIRS = POINTS // PAIR
-LEAD = 4
+PSUM_BANKS = 8
+WIDTHS = [PAIR] * (POINTS // PAIR - 1) + [PAIR // 2, PAIR // 4, PAIR // 4]
+LEAD = 6
 
 GRID_ORIGIN = -3.75
 GRID_STEP = 0.5
@@ -40,7 +41,7 @@ def tile_coords2grid_kernel(tc, coords, radii, types, offs, out):
     nc = tc.nc
     with (
         tc.tile_pool(name="held", bufs=1) as held,
-        tc.psum_pool(name="psum", bufs=PAIRS) as psum,
+        tc.psum_pool(name="psum", bufs=PSUM_BANKS) as psum,
     ):
         xyz = held.tile([ATOMS, 3], F32)
         nc.sync.dma_start(xyz[:], coords)
@@ -112,31 +113,30 @@ def tile_coords2grid_kernel(tc, coords, radii, types, offs, out):
         core = held.tile([ATOMS, POINTS], BF16)
         staged = held.tile([PICKED, POINTS], F32)
         slabs = [slice(gx * SLAB, (gx + 1) * SLAB) for gx in range(G)]
-        pairs = [slice(pair * PAIR, (pair + 1) * PAIR) for pair in range(PAIRS)]
+        ends = [sum(WIDTHS[: i + 1]) for i in range(len(WIDTHS))]
 
-        def root(gx):
+        def clamp(gx):
             nc.vector.tensor_scalar(
                 clamped[:, slabs[gx]], minus_yz[:], low[:, gx : gx + 1], high[:, gx : gx + 1], ALU.max, ALU.min
             )
-            nc.scalar.activation(
-                u_clamped[:, slabs[gx]],
-                clamped[:, slabs[gx]],
-                FN.Sqrt,
-                bias=q_x[:, gx : gx + 1],
-                scale=minus_inv_radius2[:],
-            )
 
         for gx in range(LEAD):
-            root(gx)
+            clamp(gx)
 
         picked = held.tile([ATOMS, PICKED], F32)
         nc.scalar.activation(picked[:], table[:].indirect(offsets[:]), FN.Copy)
         weights = held.tile([ATOMS, PICKED], BF16)
         nc.vector.tensor_copy(weights[:], picked[:])
 
-        sums = [psum.tile([PICKED, PAIR], F32, name="sums") for pair in range(PAIRS)]
-        for pair in range(PAIRS):
-            nc.tensor.matmul(sums[pair][:], weights[:], minus_floor[:], start=True, stop=False)
+        sums = []
+
+        def open_bank():
+            width = WIDTHS[len(sums)]
+            sums.append(psum.tile([PICKED, width], F32, name="sums"))
+            nc.tensor.matmul(sums[-1][:], weights[:], minus_floor[:, :width], start=True, stop=False)
+
+        for bank in range(PSUM_BANKS):
+            open_bank()
 
         nc.vector.tensor_scalar(
             factor[:, :, 1:STEPS],
@@ -166,21 +166,35 @@ def tile_coords2grid_kernel(tc, coords, radii, types, offs, out):
             ALU.mult,
         )
 
-        for pair in range(PAIRS):
-            for gx in (2 * pair, 2 * pair + 1):
-                if gx + LEAD < G:
-                    root(gx + LEAD)
-                nc.vector.tensor_scalar(
-                    core[:, slabs[gx]], gauss_yz[:], gauss_x[:, gx : gx + 1], FLOOR, ALU.mult, ALU.max
-                )
-            nc.tensor.matmul(sums[pair][:], weights[:], core[:, pairs[pair]], start=False, stop=False)
+        for gx in range(G):
+            if gx + LEAD < G:
+                clamp(gx + LEAD)
             nc.scalar.activation(
-                tail[:, pairs[pair]],
-                u_clamped[:, pairs[pair]],
-                FN.Square,
-                bias=3.0 * math.sqrt(FLOOR),
-                scale=-2.0 * math.sqrt(FLOOR),
+                u_clamped[:, slabs[gx]],
+                clamped[:, slabs[gx]],
+                FN.Sqrt,
+                bias=q_x[:, gx : gx + 1],
+                scale=minus_inv_radius2[:],
             )
-            nc.tensor.matmul(sums[pair][:], weights[:], tail[:, pairs[pair]], start=False, stop=True)
-            nc.any.tensor_copy(staged[:, pairs[pair]], sums[pair][:])
-            nc.sync.dma_start(out[:, pairs[pair]], staged[:, pairs[pair]])
+            nc.vector.tensor_scalar(
+                core[:, slabs[gx]], gauss_yz[:], gauss_x[:, gx : gx + 1], FLOOR, ALU.mult, ALU.max
+            )
+            for i, end in enumerate(ends):
+                if gx * SLAB < end <= (gx + 1) * SLAB:
+                    piece = slice(end - WIDTHS[i], end)
+                    nc.tensor.matmul(sums[i][:], weights[:], core[:, piece], start=False, stop=False)
+                    nc.scalar.activation(
+                        tail[:, piece],
+                        u_clamped[:, piece],
+                        FN.Square,
+                        bias=3.0 * math.sqrt(FLOOR),
+                        scale=-2.0 * math.sqrt(FLOOR),
+                    )
+                    nc.tensor.matmul(sums[i][:], weights[:], tail[:, piece], start=False, stop=True)
+                    if end <= POINTS - 2 * PAIR:
+                        nc.vector.tensor_copy(staged[:, piece], sums[i][:])
+                    else:
+                        nc.any.tensor_copy(staged[:, piece], sums[i][:])
+                    nc.sync.dma_start(out[:, piece], staged[:, piece])
+                    if len(sums) < len(WIDTHS):
+                        open_bank()

@@ -16,7 +16,7 @@ SLAB = G * G
 POINTS = G * SLAB
 PAIR = 2 * SLAB
 PSUM_BANKS = 8
-WIDTHS = [PAIR] * (POINTS // PAIR - 1) + [PAIR // 2, PAIR // 4, PAIR // 4]
+WIDTHS = [PAIR] * (POINTS // PAIR - 1) + [PAIR // 2, PAIR // 2]
 LEAD = 6
 
 GRID_ORIGIN = -3.75

import math

import concourse.mybir as mybir

F32 = mybir.dt.float32
BF16 = mybir.dt.bfloat16
U16 = mybir.dt.uint16
ALU = mybir.AluOpType
FN = mybir.ActivationFunctionType

ATOMS = 128
CHANNELS = 256
PICKED = 128
G = 16
SLAB = G * G
POINTS = G * SLAB
PAIR = 2 * SLAB
PSUM_BANKS = 8
WIDTHS = [PAIR] * (POINTS // PAIR - 1) + [PAIR // 2, PAIR // 2]
LEAD = 6

GRID_ORIGIN = -3.75
GRID_STEP = 0.5
Q_CORE = 1.0
Q_END = 2.25
FLOOR = math.exp(-2.0 * Q_CORE)

DEGREE = 6
CENTER = Q_CORE / 2.0
STEPS = DEGREE + 1

FLOPS = 2 * ATOMS * PICKED * POINTS


def power_coefficient(k):
    rest = sum(CENTER**m / math.factorial(m) for m in range(DEGREE - k + 1))
    return (-1.0) ** k / math.factorial(k) * math.exp(-CENTER) * rest


def tile_coords2grid_kernel(tc, coords, radii, types, offs, out):
    nc = tc.nc
    with (
        tc.tile_pool(name="held", bufs=1) as held,
        tc.psum_pool(name="psum", bufs=PSUM_BANKS) as psum,
    ):
        xyz = held.tile([ATOMS, 3], F32)
        nc.sync.dma_start(xyz[:], coords)
        radius = held.tile([ATOMS, 1], F32)
        nc.scalar.dma_start(radius[:], radii)
        offsets = held.tile([ATOMS, PICKED // 16], U16)
        nc.sync.dma_start(offsets[:], offs)
        table = held.tile([ATOMS, CHANNELS], F32)
        nc.scalar.dma_start(table[:], types)

        unit = held.tile([ATOMS, G], F32)
        nc.vector.memset(unit[:], 1.0)
        pitch = held.tile([ATOMS, G], F32)
        nc.vector.memset(pitch[:], GRID_STEP)
        axis = held.tile([ATOMS, G], F32)
        nc.vector.tensor_tensor_scan(axis[:], unit[:], pitch[:], GRID_ORIGIN - GRID_STEP, ALU.mult, ALU.add)

        one = held.tile([ATOMS, 1], F32)
        nc.vector.memset(one[:], 1.0)
        warm = held.tile([ATOMS, 1], F32)
        nc.scalar.activation(warm[:], one[:], FN.Sqrt)

        series = held.tile([ATOMS, STEPS], F32)
        for step in range(STEPS):
            nc.vector.memset(series[:, step : step + 1], power_coefficient(DEGREE - step))
        coefficient = held.tile([ATOMS, 3 * G, STEPS], F32)
        nc.vector.tensor_copy(coefficient[:], series[:].unsqueeze(1).to_broadcast([ATOMS, 3 * G, STEPS]))
        factor = held.tile([ATOMS, 3 * G, STEPS], F32)
        nc.vector.memset(factor[:], 0.0)

        nothing = held.tile([ATOMS, 1], F32)
        nc.vector.memset(nothing[:], 0.0)
        minus_floor = held.tile([ATOMS, PAIR], BF16)
        nc.vector.tensor_scalar(
            minus_floor[:], nothing[:].to_broadcast([ATOMS, PAIR]), FLOOR, -1.0, ALU.max, ALU.mult
        )

        dist2 = held.tile([ATOMS, 3, G], F32)
        for k in range(3):
            nc.scalar.activation(dist2[:, k, :], axis[:], FN.Square, bias=xyz[:, k : k + 1], scale=-1.0)
        dist2_x = dist2[:, 0, :]
        core2 = held.tile([ATOMS, 1], F32)
        nc.vector.scalar_tensor_tensor(core2[:], radius[:], Q_CORE, radius[:], op0=ALU.mult, op1=ALU.mult)
        end2 = held.tile([ATOMS, 1], F32)
        nc.vector.scalar_tensor_tensor(end2[:], radius[:], Q_END, radius[:], op0=ALU.mult, op1=ALU.mult)
        minus_yz = held.tile([ATOMS, SLAB], F32)
        nc.vector.scalar_tensor_tensor(
            minus_yz[:].rearrange("n (y z) -> n y z", y=G),
            dist2[:, 1, :].unsqueeze(2).to_broadcast([ATOMS, G, G]),
            -1.0,
            dist2[:, 2, :].unsqueeze(1).to_broadcast([ATOMS, G, G]),
            op0=ALU.mult,
            op1=ALU.subtract,
        )
        low = held.tile([ATOMS, G], F32)
        nc.vector.tensor_scalar(low[:], dist2_x, end2[:], 0.0, ALU.subtract, ALU.min)
        high = held.tile([ATOMS, G], F32)
        nc.vector.tensor_scalar_sub(high[:], dist2_x, core2[:])
        inv_radius2 = held.tile([ATOMS, 1], F32)
        nc.vector.reciprocal(inv_radius2[:], core2[:])
        minus_inv_radius2 = held.tile([ATOMS, 1], F32)
        nc.vector.tensor_scalar_mul(minus_inv_radius2[:], inv_radius2[:], -1.0)
        q_x = held.tile([ATOMS, G], F32)
        nc.vector.tensor_scalar(q_x[:], dist2_x, end2[:], inv_radius2[:], ALU.min, ALU.mult)

        clamped = held.tile([ATOMS, POINTS], F32)
        u_clamped = held.tile([ATOMS, POINTS], F32)
        tail = held.tile([ATOMS, POINTS], BF16)
        core = held.tile([ATOMS, POINTS], BF16)
        staged = held.tile([PICKED, POINTS], F32)
        slabs = [slice(gx * SLAB, (gx + 1) * SLAB) for gx in range(G)]
        ends = [sum(WIDTHS[: i + 1]) for i in range(len(WIDTHS))]

        def clamp(gx):
            nc.vector.tensor_scalar(
                clamped[:, slabs[gx]], minus_yz[:], low[:, gx : gx + 1], high[:, gx : gx + 1], ALU.max, ALU.min
            )

        for gx in range(LEAD):
            clamp(gx)

        picked = held.tile([ATOMS, PICKED], F32)
        nc.scalar.activation(picked[:], table[:].indirect(offsets[:]), FN.Copy)
        weights = held.tile([ATOMS, PICKED], BF16)
        nc.vector.tensor_copy(weights[:], picked[:])

        sums = []

        def open_bank():
            width = WIDTHS[len(sums)]
            sums.append(psum.tile([PICKED, width], F32, name="sums"))
            nc.tensor.matmul(sums[-1][:], weights[:], minus_floor[:, :width], start=True, stop=False)

        for bank in range(PSUM_BANKS):
            open_bank()

        nc.vector.tensor_scalar(
            factor[:, :, 1:STEPS],
            dist2[:].rearrange("n k g -> n (k g)").unsqueeze(2).to_broadcast([ATOMS, 3 * G, DEGREE]),
            end2[:],
            inv_radius2[:],
            ALU.min,
            ALU.mult,
        )
        horner = held.tile([ATOMS, 3, G, STEPS], F32)
        nc.vector.tensor_tensor_scan(
            horner[:].rearrange("n k g s -> n (k g s)"),
            factor[:].rearrange("n t s -> n (t s)"),
            coefficient[:].rearrange("n t s -> n (t s)"),
            0.0,
            ALU.mult,
            ALU.add,
        )
        gauss_axis = held.tile([ATOMS, 3, G], F32)
        nc.vector.tensor_tensor(gauss_axis[:], horner[:, :, :, DEGREE], horner[:, :, :, DEGREE], ALU.mult)
        gauss_x = gauss_axis[:, 0, :]
        gauss_yz = held.tile([ATOMS, SLAB], F32)
        nc.vector.tensor_tensor(
            gauss_yz[:].rearrange("n (y z) -> n y z", y=G),
            gauss_axis[:, 1, :].unsqueeze(2).to_broadcast([ATOMS, G, G]),
            gauss_axis[:, 2, :].unsqueeze(1).to_broadcast([ATOMS, G, G]),
            ALU.mult,
        )

        for gx in range(G):
            if gx + LEAD < G:
                clamp(gx + LEAD)
            nc.scalar.activation(
                u_clamped[:, slabs[gx]],
                clamped[:, slabs[gx]],
                FN.Sqrt,
                bias=q_x[:, gx : gx + 1],
                scale=minus_inv_radius2[:],
            )
            nc.vector.tensor_scalar(
                core[:, slabs[gx]], gauss_yz[:], gauss_x[:, gx : gx + 1], FLOOR, ALU.mult, ALU.max
            )
            for i, end in enumerate(ends):
                if gx * SLAB < end <= (gx + 1) * SLAB:
                    piece = slice(end - WIDTHS[i], end)
                    nc.tensor.matmul(sums[i][:], weights[:], core[:, piece], start=False, stop=False)
                    nc.scalar.activation(
                        tail[:, piece],
                        u_clamped[:, piece],
                        FN.Square,
                        bias=3.0 * math.sqrt(FLOOR),
                        scale=-2.0 * math.sqrt(FLOOR),
                    )
                    nc.tensor.matmul(sums[i][:], weights[:], tail[:, piece], start=False, stop=True)
                    if end <= POINTS - 2 * PAIR:
                        nc.vector.tensor_copy(staged[:, piece], sums[i][:])
                    else:
                        nc.any.tensor_copy(staged[:, piece], sums[i][:])
                    nc.sync.dma_start(out[:, piece], staged[:, piece])
                    if len(sums) < len(WIDTHS):
                        open_bank()
